import numpy as np
import ml_dtypes


def mxq(x, axis, fmt="e4m3"):
    dtype, down = {"e4m3": (ml_dtypes.float8_e4m3fn, 7), "e5m2": (ml_dtypes.float8_e5m2, 14)}[fmt]
    v = np.moveaxis(np.asarray(x, np.float32).astype(ml_dtypes.bfloat16).astype(np.float64), axis, -1)
    blocks = v.reshape(v.shape[:-1] + (-1, 32))
    amax = np.abs(blocks).max(-1, keepdims=True)
    byte = np.maximum(np.where(amax > 0, np.frexp(amax)[1] - 1 + 127, 0) - down, 1)
    scale = np.exp2(byte - 127.0)
    codes = (blocks / scale).astype(np.float32).astype(dtype).astype(np.float64)
    return np.moveaxis((codes * scale).reshape(v.shape), -1, axis)


WIDE = False


def mx_kscale(k):
    if not WIDE:
        return np.ones(k)
    levels = np.array([10, -10, 5, -5, 0])
    a = np.random.permutation(np.resize(levels, k // 512 * 4)).reshape(k // 512, 4)
    idx = np.arange(k)
    return np.exp2(a[idx // 512, idx % 128 // 32])


BF16 = ml_dtypes.bfloat16


def bf(x):
    return np.asarray(x, np.float32).astype(BF16)


def f64(x):
    return np.asarray(x).astype(np.float64)


B, C, H, W = 1, 1024, 64, 128
CK, CV = C // 8, C // 2
HP, WP = H // 2, W // 2
N, M = H * W, HP * WP


def maxpool2x2(v):
    return v.reshape(v.shape[0], v.shape[1], HP, 2, WP, 2).max(axis=(3, 5))


def setup_inputs():
    s = mx_kscale(C)
    a = 1.7 / CK ** 0.25
    return {"x": bf(np.random.standard_normal((B, C, H, W)) * s[:, None, None]),
            "w_phi": bf(np.random.standard_normal((CK, C)) * a / np.sqrt(C) / s),
            "w_g": bf(np.random.standard_normal((CV, C)) / np.sqrt(C) / s)}


def reference(x, w_phi, w_g):
    xq = mxq(f64(x).reshape(B, C, N), 1, "e4m3")
    u_phi = (mxq(f64(w_phi), 1, "e4m3") @ xq).reshape(B, CK, H, W)
    u_g = (mxq(f64(w_g), 1, "e4m3") @ xq).reshape(B, CV, H, W)
    phi = maxpool2x2(u_phi).reshape(B, CK, M)
    g = maxpool2x2(u_g).reshape(B, CV, M)
    return phi, g

@@ -1,0 +1,134 @@
+from contextlib import ExitStack
+
+import concourse.mybir as mybir
+from concourse.masks import make_identity
+
+BF16 = mybir.dt.bfloat16
+F32 = mybir.dt.float32
+U32 = mybir.dt.uint32
+U8 = mybir.dt.uint8
+FP8X4 = mybir.dt.float8_e4m3fn_x4
+
+P = 128
+PACK = 4
+K_PASS = P * PACK
+
+CHANNELS, HEIGHT, WIDTH = 1024, 64, 128
+PIXELS = HEIGHT * WIDTH
+PASSES = CHANNELS // K_PASS
+M_TILES = 5
+G_TILES = M_TILES - 1
+
+N_TILE = 512
+CHUNKS = PIXELS // N_TILE
+ROWS_PER_CHUNK = N_TILE // WIDTH
+POOLED_ROWS = ROWS_PER_CHUNK // 2
+POOLED_WIDTH = WIDTH // 2
+POOLED_TILE = POOLED_ROWS * POOLED_WIDTH
+
+CHUNKS_PER_LOAD = 2
+LOAD_COLS = CHUNKS_PER_LOAD * N_TILE
+LOAD_GROUPS = CHUNKS // CHUNKS_PER_LOAD
+CHUNKS_PER_STORE = 2
+STORE_COLS = CHUNKS_PER_STORE * POOLED_TILE
+
+RUN = 4
+HEAD_CHUNKS = 4
+
+FLOPS = 2 * M_TILES * P * CHANNELS * PIXELS
+
+
+def tile_attention_pa_t_kernel(tc, x, w_phi, w_g, out_0, out_1):
+    nc = tc.nc
+    with ExitStack() as ctx:
+        const = ctx.enter_context(tc.tile_pool(name="const", bufs=1))
+        raw_pool = ctx.enter_context(tc.tile_pool(name="raw", bufs=LOAD_GROUPS * PASSES))
+        stream = ctx.enter_context(tc.tile_pool(name="stream", bufs=3))
+        psum = ctx.enter_context(tc.psum_pool(name="psum", bufs=8))
+
+        x_rows = x[0].rearrange("(g p j) h w -> g p j (h w)", g=PASSES, p=P, j=PACK)
+        raw = {}
+
+        def load_x(group):
+            for g in range(PASSES):
+                raw_tile = raw_pool.tile([P, PACK, LOAD_COLS], BF16, tag="raw")
+                cols = slice(group * LOAD_COLS, (group + 1) * LOAD_COLS)
+                nc.sync.dma_start(out=raw_tile[:], in_=x_rows[g, :, :, cols])
+                raw[(group, g)] = raw_tile
+
+        load_x(0)
+        w_rows = const.tile([P, M_TILES, CHANNELS], BF16)
+        nc.sync.dma_start(out=w_rows[:, 0, :], in_=w_phi)
+        nc.sync.dma_start(out=w_rows[:, 1:M_TILES, :], in_=w_g.rearrange("(m o) c -> o m c", o=P))
+        for group in range(1, LOAD_GROUPS):
+            load_x(group)
+
+        identity = const.tile([P, P], F32)
+        make_identity(nc, identity[:])
+        w_words = w_rows[:].bitcast(F32).rearrange("o m (g p u) -> o m g u p", g=PASSES, p=P, u=2)
+        w_grouped = const.tile([P, M_TILES, PASSES, P, PACK], BF16, align_bytes=64)
+        w_grouped_words = w_grouped[:].bitcast(F32)
+        w_codes = const.tile([P, M_TILES, PASSES, P], U32, align_bytes=64)
+        w_scales = const.tile([P, M_TILES, PASSES, P], U8, align_bytes=64)
+        for m in range(M_TILES):
+            w_bank = psum.tile([P, PASSES, 2, P], F32, tag="bank")
+            for g in range(PASSES):
+                for u in range(2):
+                    nc.tensor.transpose(w_bank[:, g, u, :], w_words[:, m, g, u, :], identity[:])
+            nc.vector.tensor_copy(out=w_grouped_words[:, m], in_=w_bank[:].rearrange("p g u o -> p g o u"))
+        for m in range(M_TILES):
+            nc.vector.quantize_mx(
+                out=w_codes[:, m].rearrange("p g o -> p (g o)").bitcast(FP8X4),
+                scales=w_scales[:, m].rearrange("p g o -> p (g o)"),
+                in_=w_grouped[:, m].rearrange("p g o t -> p (g o t)"),
+            )
+
+        phi_out = out_0[0]
+        g_out = out_1[0].rearrange("(m o) n -> o m n", o=P)
+        pooled = None
+        for chunk in range(CHUNKS):
+            group, part = divmod(chunk, CHUNKS_PER_LOAD)
+            cols = slice(part * N_TILE, (part + 1) * N_TILE)
+
+            grouped = stream.tile([P, PASSES, N_TILE, PACK], BF16, align_bytes=64)
+            for g in range(PASSES):
+                copy = nc.vector.tensor_copy if (chunk < HEAD_CHUNKS and g == 1) else nc.scalar.copy
+                copy(
+                    out=grouped[:, g].rearrange("p (c i) t -> p c t i", i=RUN),
+                    in_=raw[(group, g)][:, :, cols].rearrange("p t (c i) -> p c t i", i=RUN),
+                )
+
+            codes = stream.tile([P, PASSES, N_TILE], U32, align_bytes=64)
+            scales = stream.tile([P, PASSES, N_TILE], U8, align_bytes=64)
+            nc.vector.quantize_mx(
+                out=codes[:].rearrange("p g n -> p (g n)").bitcast(FP8X4),
+                scales=scales[:].rearrange("p g n -> p (g n)"),
+                in_=grouped[:].rearrange("p g n t -> p (g n t)"),
+            )
+
+            if chunk % CHUNKS_PER_STORE == 0:
+                pooled = stream.tile([P, M_TILES, STORE_COLS], F32)
+            first = (chunk % CHUNKS_PER_STORE) * POOLED_TILE
+            for m in range(M_TILES):
+                bank = psum.tile([P, N_TILE], F32, tag="bank")
+                for g in range(PASSES):
+                    nc.tensor.matmul_mx(
+                        out=bank[:],
+                        lhsT=w_codes[:, m, g, :].bitcast(FP8X4),
+                        lhsT_scale=w_scales[:, m, g, :],
+                        rhs=codes[:, g, :].bitcast(FP8X4),
+                        rhs_scale=scales[:, g, :],
+                        start=(g == 0),
+                        stop=(g == PASSES - 1),
+                    )
+                nc.vector.tensor_reduce(
+                    out=pooled[:, m, first : first + POOLED_TILE].rearrange("p (i j) -> p i j", i=POOLED_ROWS),
+                    in_=bank[:].rearrange("p (i a j b) -> p i j a b", i=POOLED_ROWS, a=2, j=POOLED_WIDTH, b=2),
+                    axis=mybir.AxisListType.XY,
+                    op=mybir.AluOpType.max,
+                )
+
+            if chunk % CHUNKS_PER_STORE == CHUNKS_PER_STORE - 1:
+                done = (chunk // CHUNKS_PER_STORE) * STORE_COLS
+                nc.sync.dma_start(out=phi_out[:, done : done + STORE_COLS], in_=pooled[:, 0, :])
+                nc.sync.dma_start(out=g_out[:, :, done : done + STORE_COLS], in_=pooled[:, 1:M_TILES, :])

@@ -38,6 +38,14 @@ HEAD_CHUNKS = 4
 FLOPS = 2 * M_TILES * P * CHANNELS * PIXELS
 
 
+def quantise_weights(nc, w_codes, w_scales, w_grouped, m):
+    nc.vector.quantize_mx(
+        out=w_codes[:, m].rearrange("p g o -> p (g o)").bitcast(FP8X4),
+        scales=w_scales[:, m].rearrange("p g o -> p (g o)"),
+        in_=w_grouped[:, m].rearrange("p g o t -> p (g o t)"),
+    )
+
+
 def tile_attention_pa_t_kernel(tc, x, w_phi, w_g, out_0, out_1):
     nc = tc.nc
     with ExitStack() as ctx:
@@ -45,23 +53,20 @@ def tile_attention_pa_t_kernel(tc, x, w_phi, w_g, out_0, out_1):
         raw_pool = ctx.enter_context(tc.tile_pool(name="raw", bufs=LOAD_GROUPS * PASSES))
         stream = ctx.enter_context(tc.tile_pool(name="stream", bufs=3))
         psum = ctx.enter_context(tc.psum_pool(name="psum", bufs=8))
+        ctx.enter_context(tc.manual_schedule())
 
-        x_rows = x[0].rearrange("(g p j) h w -> g p j (h w)", g=PASSES, p=P, j=PACK)
-        raw = {}
-
-        def load_x(group):
-            for g in range(PASSES):
-                raw_tile = raw_pool.tile([P, PACK, LOAD_COLS], BF16, tag="raw")
-                cols = slice(group * LOAD_COLS, (group + 1) * LOAD_COLS)
-                nc.sync.dma_start(out=raw_tile[:], in_=x_rows[g, :, :, cols])
-                raw[(group, g)] = raw_tile
-
-        load_x(0)
         w_rows = const.tile([P, M_TILES, CHANNELS], BF16)
         nc.sync.dma_start(out=w_rows[:, 0, :], in_=w_phi)
         nc.sync.dma_start(out=w_rows[:, 1:M_TILES, :], in_=w_g.rearrange("(m o) c -> o m c", o=P))
-        for group in range(1, LOAD_GROUPS):
-            load_x(group)
+        x_rows = x[0].rearrange("(g p j) h w -> g p j (h w)", g=PASSES, p=P, j=PACK)
+        raw = {}
+        for group in range(LOAD_GROUPS):
+            for g in range(PASSES):
+                raw_tile = raw_pool.tile([P, PACK, LOAD_COLS], BF16, tag="raw")
+                nc.sync.dma_start(
+                    out=raw_tile[:], in_=x_rows[g, :, :, group * LOAD_COLS : (group + 1) * LOAD_COLS]
+                )
+                raw[(group, g)] = raw_tile
 
         identity = const.tile([P, P], F32)
         make_identity(nc, identity[:])
@@ -76,59 +81,82 @@ def tile_attention_pa_t_kernel(tc, x, w_phi, w_g, out_0, out_1):
                 for u in range(2):
                     nc.tensor.transpose(w_bank[:, g, u, :], w_words[:, m, g, u, :], identity[:])
             nc.vector.tensor_copy(out=w_grouped_words[:, m], in_=w_bank[:].rearrange("p g u o -> p g o u"))
-        for m in range(M_TILES):
-            nc.vector.quantize_mx(
-                out=w_codes[:, m].rearrange("p g o -> p (g o)").bitcast(FP8X4),
-                scales=w_scales[:, m].rearrange("p g o -> p (g o)"),
-                in_=w_grouped[:, m].rearrange("p g o t -> p (g o t)"),
-            )
+            if m >= 1:
+                quantise_weights(nc, w_codes, w_scales, w_grouped, m - 1)
+        quantise_weights(nc, w_codes, w_scales, w_grouped, M_TILES - 1)
 
         phi_out = out_0[0]
         g_out = out_1[0].rearrange("(m o) n -> o m n", o=P)
-        pooled = None
-        for chunk in range(CHUNKS):
+        grouped, codes, scales, banks, pooled = {}, {}, {}, {}, {}
+
+        def regroup(chunk):
             group, part = divmod(chunk, CHUNKS_PER_LOAD)
-            cols = slice(part * N_TILE, (part + 1) * N_TILE)
-
-            grouped = stream.tile([P, PASSES, N_TILE, PACK], BF16, align_bytes=64)
+            grouped_tile = stream.tile([P, PASSES, N_TILE, PACK], BF16, tag="grouped", align_bytes=64)
+            by_vector = chunk < HEAD_CHUNKS and chunk % 2 == 1
+            copy = nc.vector.tensor_copy if by_vector else nc.scalar.copy
             for g in range(PASSES):
-                copy = nc.vector.tensor_copy if (chunk < HEAD_CHUNKS and g == 1) else nc.scalar.copy
                 copy(
-                    out=grouped[:, g].rearrange("p (c i) t -> p c t i", i=RUN),
-                    in_=raw[(group, g)][:, :, cols].rearrange("p t (c i) -> p c t i", i=RUN),
+                    out=grouped_tile[:, g].rearrange("p (c i) t -> p c t i", i=RUN),
+                    in_=raw[(group, g)][:, :, part * N_TILE : (part + 1) * N_TILE].rearrange(
+                        "p t (c i) -> p c t i", i=RUN
+                    ),
                 )
+            grouped[chunk] = grouped_tile
 
-            codes = stream.tile([P, PASSES, N_TILE], U32, align_bytes=64)
-            scales = stream.tile([P, PASSES, N_TILE], U8, align_bytes=64)
+        def quantise(chunk):
+            codes_tile = stream.tile([P, PASSES, N_TILE], U32, tag="codes", align_bytes=64)
+            scales_tile = stream.tile([P, PASSES, N_TILE], U8, tag="scales", align_bytes=64)
             nc.vector.quantize_mx(
-                out=codes[:].rearrange("p g n -> p (g n)").bitcast(FP8X4),
-                scales=scales[:].rearrange("p g n -> p (g n)"),
-                in_=grouped[:].rearrange("p g n t -> p (g n t)"),
+                out=codes_tile[:].rearrange("p g n -> p (g n)").bitcast(FP8X4),
+                scales=scales_tile[:].rearrange("p g n -> p (g n)"),
+                in_=grouped[chunk][:].rearrange("p g n t -> p (g n t)"),
+            )
+            codes[chunk], scales[chunk] = codes_tile, scales_tile
+
+        def multiply(chunk, m):
+            bank = psum.tile([P, N_TILE], F32, tag="bank")
+            for g in range(PASSES):
+                nc.tensor.matmul_mx(
+                    out=bank[:],
+                    lhsT=w_codes[:, m, g, :].bitcast(FP8X4),
+                    lhsT_scale=w_scales[:, m, g, :],
+                    rhs=codes[chunk][:, g, :].bitcast(FP8X4),
+                    rhs_scale=scales[chunk][:, g, :],
+                    start=(g == 0),
+                    stop=(g == PASSES - 1),
+                )
+            banks[(chunk, m)] = bank
+
+        def pool(chunk, m):
+            batch, part = divmod(chunk, CHUNKS_PER_STORE)
+            if part == 0 and m == 0:
+                pooled_tile = stream.tile([P, M_TILES, STORE_COLS], F32, tag="pooled")
+                pooled[batch] = pooled_tile
+            nc.vector.tensor_reduce(
+                out=pooled[batch][:, m, part * POOLED_TILE : (part + 1) * POOLED_TILE].rearrange(
+                    "p (i j) -> p i j", i=POOLED_ROWS
+                ),
+                in_=banks[(chunk, m)][:].rearrange(
+                    "p (i a j b) -> p i j a b", i=POOLED_ROWS, a=2, j=POOLED_WIDTH, b=2
+                ),
+                axis=mybir.AxisListType.XY,
+                op=mybir.AluOpType.max,
             )
 
-            if chunk % CHUNKS_PER_STORE == 0:
-                pooled = stream.tile([P, M_TILES, STORE_COLS], F32)
-            first = (chunk % CHUNKS_PER_STORE) * POOLED_TILE
-            for m in range(M_TILES):
-                bank = psum.tile([P, N_TILE], F32, tag="bank")
-                for g in range(PASSES):
-                    nc.tensor.matmul_mx(
-                        out=bank[:],
-                        lhsT=w_codes[:, m, g, :].bitcast(FP8X4),
-                        lhsT_scale=w_scales[:, m, g, :],
-                        rhs=codes[:, g, :].bitcast(FP8X4),
-                        rhs_scale=scales[:, g, :],
-                        start=(g == 0),
-                        stop=(g == PASSES - 1),
-                    )
-                nc.vector.tensor_reduce(
-                    out=pooled[:, m, first : first + POOLED_TILE].rearrange("p (i j) -> p i j", i=POOLED_ROWS),
-                    in_=bank[:].rearrange("p (i a j b) -> p i j a b", i=POOLED_ROWS, a=2, j=POOLED_WIDTH, b=2),
-                    axis=mybir.AxisListType.XY,
-                    op=mybir.AluOpType.max,
-                )
+        def store(batch):
+            cols = slice(batch * STORE_COLS, (batch + 1) * STORE_COLS)
+            nc.sync.dma_start(out=phi_out[:, cols], in_=pooled[batch][:, 0, :])
+            nc.sync.dma_start(out=g_out[:, :, cols], in_=pooled[batch][:, 1:M_TILES, :])
 
-            if chunk % CHUNKS_PER_STORE == CHUNKS_PER_STORE - 1:
-                done = (chunk // CHUNKS_PER_STORE) * STORE_COLS
-                nc.sync.dma_start(out=phi_out[:, done : done + STORE_COLS], in_=pooled[:, 0, :])
-                nc.sync.dma_start(out=g_out[:, :, done : done + STORE_COLS], in_=pooled[:, 1:M_TILES, :])
+        for step in range(-2, CHUNKS + 1):
+            if step + 2 < CHUNKS:
+                regroup(step + 2)
+            if 0 <= step + 1 < CHUNKS:
+                quantise(step + 1)
+            for m in range(M_TILES):
+                if step >= 1:
+                    pool(step - 1, m)
+                if 0 <= step < CHUNKS:
+                    multiply(step, m)
+            if step >= 1 and step % CHUNKS_PER_STORE == 0:
+                store(step // CHUNKS_PER_STORE - 1)

@@ -8,6 +8,7 @@ F32 = mybir.dt.float32
 U32 = mybir.dt.uint32
 U8 = mybir.dt.uint8
 FP8X4 = mybir.dt.float8_e4m3fn_x4
+MAX = mybir.AluOpType.max
 
 P = 128
 PACK = 4
@@ -17,12 +18,10 @@ CHANNELS, HEIGHT, WIDTH = 1024, 64, 128
 PIXELS = HEIGHT * WIDTH
 PASSES = CHANNELS // K_PASS
 M_TILES = 5
-G_TILES = M_TILES - 1
 
 N_TILE = 512
 CHUNKS = PIXELS // N_TILE
-ROWS_PER_CHUNK = N_TILE // WIDTH
-POOLED_ROWS = ROWS_PER_CHUNK // 2
+POOLED_ROWS = N_TILE // WIDTH // 2
 POOLED_WIDTH = WIDTH // 2
 POOLED_TILE = POOLED_ROWS * POOLED_WIDTH
 
@@ -33,7 +32,10 @@ CHUNKS_PER_STORE = 2
 STORE_COLS = CHUNKS_PER_STORE * POOLED_TILE
 
 RUN = 4
-HEAD_CHUNKS = 4
+GPSIMD_COLS = 384
+SCALAR_COLS = N_TILE - GPSIMD_COLS
+SHARED_TILES = 2
+PLAIN_TILES = M_TILES - SHARED_TILES
 
 FLOPS = 2 * M_TILES * P * CHANNELS * PIXELS
 
@@ -50,23 +52,31 @@ def tile_attention_pa_t_kernel(tc, x, w_phi, w_g, out_0, out_1):
     nc = tc.nc
     with ExitStack() as ctx:
         const = ctx.enter_context(tc.tile_pool(name="const", bufs=1))
-        raw_pool = ctx.enter_context(tc.tile_pool(name="raw", bufs=LOAD_GROUPS * PASSES))
+        raw_pool = ctx.enter_context(tc.tile_pool(name="raw", bufs=1))
         stream = ctx.enter_context(tc.tile_pool(name="stream", bufs=3))
         psum = ctx.enter_context(tc.psum_pool(name="psum", bufs=8))
         ctx.enter_context(tc.manual_schedule())
 
         w_rows = const.tile([P, M_TILES, CHANNELS], BF16)
         nc.sync.dma_start(out=w_rows[:, 0, :], in_=w_phi)
-        nc.sync.dma_start(out=w_rows[:, 1:M_TILES, :], in_=w_g.rearrange("(m o) c -> o m c", o=P))
+        for m in range(1, M_TILES):
+            nc.sync.dma_start(out=w_rows[:, m, :], in_=w_g[(m - 1) * P : m * P, :])
         x_rows = x[0].rearrange("(g p j) h w -> g p j (h w)", g=PASSES, p=P, j=PACK)
         raw = {}
-        for group in range(LOAD_GROUPS):
+
+        def load_x(first_chunk, chunks, tag, bufs):
             for g in range(PASSES):
-                raw_tile = raw_pool.tile([P, PACK, LOAD_COLS], BF16, tag="raw")
+                raw_tile = raw_pool.tile([P, PACK, chunks * N_TILE], BF16, tag=tag, bufs=bufs)
                 nc.sync.dma_start(
-                    out=raw_tile[:], in_=x_rows[g, :, :, group * LOAD_COLS : (group + 1) * LOAD_COLS]
+                    out=raw_tile[:], in_=x_rows[g, :, :, first_chunk * N_TILE : (first_chunk + chunks) * N_TILE]
                 )
-                raw[(group, g)] = raw_tile
+                for part in range(chunks):
+                    raw[(first_chunk + part, g)] = raw_tile[:, :, part * N_TILE : (part + 1) * N_TILE]
+
+        for chunk in range(CHUNKS_PER_LOAD):
+            load_x(chunk, 1, "raw_chunk", CHUNKS_PER_LOAD * PASSES)
+        for group in range(1, LOAD_GROUPS):
+            load_x(group * CHUNKS_PER_LOAD, CHUNKS_PER_LOAD, "raw_group", (LOAD_GROUPS - 1) * PASSES)
 
         identity = const.tile([P, P], F32)
         make_identity(nc, identity[:])
@@ -87,20 +97,23 @@ def tile_attention_pa_t_kernel(tc, x, w_phi, w_g, out_0, out_1):
 
         phi_out = out_0[0]
         g_out = out_1[0].rearrange("(m o) n -> o m n", o=P)
-        grouped, codes, scales, banks, pooled = {}, {}, {}, {}, {}
+        grouped, codes, scales, banks, upper, pooled = {}, {}, {}, {}, {}, {}
 
         def regroup(chunk):
-            group, part = divmod(chunk, CHUNKS_PER_LOAD)
             grouped_tile = stream.tile([P, PASSES, N_TILE, PACK], BF16, tag="grouped", align_bytes=64)
-            by_vector = chunk < HEAD_CHUNKS and chunk % 2 == 1
-            copy = nc.vector.tensor_copy if by_vector else nc.scalar.copy
-            for g in range(PASSES):
-                copy(
-                    out=grouped_tile[:, g].rearrange("p (c i) t -> p c t i", i=RUN),
-                    in_=raw[(group, g)][:, :, part * N_TILE : (part + 1) * N_TILE].rearrange(
-                        "p t (c i) -> p c t i", i=RUN
-                    ),
+            for g, cols in ((0, N_TILE), (1, SCALAR_COLS)):
+                nc.scalar.copy(
+                    out=grouped_tile[:, g, 0:cols, :].rearrange("p (c i) t -> p c t i", i=RUN),
+                    in_=raw[(chunk, g)][:, :, 0:cols].rearrange("p t (c i) -> p c t i", i=RUN),
                 )
+            nc.gpsimd.tensor_scalar(
+                out=grouped_tile[:, 1, SCALAR_COLS:N_TILE, :],
+                in0=raw[(chunk, 1)][:, :, SCALAR_COLS:N_TILE].rearrange("p t n -> p n t"),
+                scalar1=1.0,
+                scalar2=0.0,
+                op0=mybir.AluOpType.mult,
+                op1=mybir.AluOpType.add,
+            )
             grouped[chunk] = grouped_tile
 
         def quantise(chunk):
@@ -127,20 +140,39 @@ def tile_attention_pa_t_kernel(tc, x, w_phi, w_g, out_0, out_1):
                 )
             banks[(chunk, m)] = bank
 
-        def pool(chunk, m):
+        def pooled_slice(chunk):
             batch, part = divmod(chunk, CHUNKS_PER_STORE)
-            if part == 0 and m == 0:
+            return pooled[batch][:, :, part * POOLED_TILE : (part + 1) * POOLED_TILE]
+
+        def copy_upper_rows(chunk):
+            upper_tile = stream.tile([P, SHARED_TILES, POOLED_ROWS, WIDTH], F32, tag="upper")
+            for k in range(SHARED_TILES):
+                rows = banks[(chunk, PLAIN_TILES + k)][:].rearrange("p (i a w) -> p i a w", i=POOLED_ROWS, a=2)
+                nc.scalar.copy(out=upper_tile[:, k], in_=rows[:, :, 0, :])
+            upper[chunk] = upper_tile
+
+        def pool_bank(chunk, m):
+            if chunk % CHUNKS_PER_STORE == 0 and m == 0:
                 pooled_tile = stream.tile([P, M_TILES, STORE_COLS], F32, tag="pooled")
-                pooled[batch] = pooled_tile
-            nc.vector.tensor_reduce(
-                out=pooled[batch][:, m, part * POOLED_TILE : (part + 1) * POOLED_TILE].rearrange(
-                    "p (i j) -> p i j", i=POOLED_ROWS
-                ),
-                in_=banks[(chunk, m)][:].rearrange(
-                    "p (i a j b) -> p i j a b", i=POOLED_ROWS, a=2, j=POOLED_WIDTH, b=2
-                ),
-                axis=mybir.AxisListType.XY,
-                op=mybir.AluOpType.max,
+                pooled[chunk // CHUNKS_PER_STORE] = pooled_tile
+            if m < PLAIN_TILES:
+                nc.vector.tensor_reduce(
+                    out=pooled_slice(chunk)[:, m, :].rearrange("p (i j) -> p i j", i=POOLED_ROWS),
+                    in_=banks[(chunk, m)][:].rearrange(
+                        "p (i a j b) -> p i j a b", i=POOLED_ROWS, a=2, j=POOLED_WIDTH, b=2
+                    ),
+                    axis=mybir.AxisListType.XY,
+                    op=MAX,
+                )
+            else:
+                k = m - PLAIN_TILES
+                rows = banks[(chunk, m)][:].rearrange("p (i a w) -> p i a w", i=POOLED_ROWS, a=2)
+                nc.vector.tensor_tensor(out=upper[chunk][:, k], in0=rows[:, :, 1, :], in1=upper[chunk][:, k], op=MAX)
+
+        def pool_columns(chunk):
+            pairs = upper[chunk][:].rearrange("p k i (j b) -> p k (i j) b", b=2)
+            nc.vector.tensor_tensor(
+                out=pooled_slice(chunk)[:, PLAIN_TILES:M_TILES, :], in0=pairs[:, :, :, 0], in1=pairs[:, :, :, 1], op=MAX
             )
 
         def store(batch):
@@ -148,15 +180,19 @@ def tile_attention_pa_t_kernel(tc, x, w_phi, w_g, out_0, out_1):
             nc.sync.dma_start(out=phi_out[:, cols], in_=pooled[batch][:, 0, :])
             nc.sync.dma_start(out=g_out[:, :, cols], in_=pooled[batch][:, 1:M_TILES, :])
 
-        for step in range(-2, CHUNKS + 1):
-            if step + 2 < CHUNKS:
-                regroup(step + 2)
+        for step in range(-2, CHUNKS + 2):
             if 0 <= step + 1 < CHUNKS:
                 quantise(step + 1)
+            if step >= 2:
+                pool_columns(step - 2)
+                if (step - 2) % CHUNKS_PER_STORE == CHUNKS_PER_STORE - 1:
+                    store((step - 2) // CHUNKS_PER_STORE)
+            if 1 <= step <= CHUNKS:
+                copy_upper_rows(step - 1)
+            if step + 2 < CHUNKS:
+                regroup(step + 2)
             for m in range(M_TILES):
-                if step >= 1:
-                    pool(step - 1, m)
+                if 1 <= step <= CHUNKS:
+                    pool_bank(step - 1, m)
                 if 0 <= step < CHUNKS:
                     multiply(step, m)
-            if step >= 1 and step % CHUNKS_PER_STORE == 0:
-                store(step // CHUNKS_PER_STORE - 1)

@@ -28,14 +28,11 @@ POOLED_TILE = POOLED_ROWS * POOLED_WIDTH
 CHUNKS_PER_LOAD = 2
 LOAD_COLS = CHUNKS_PER_LOAD * N_TILE
 LOAD_GROUPS = CHUNKS // CHUNKS_PER_LOAD
-CHUNKS_PER_STORE = 2
-STORE_COLS = CHUNKS_PER_STORE * POOLED_TILE
 
 RUN = 4
-GPSIMD_COLS = 384
+GPSIMD_COLS = 320
 SCALAR_COLS = N_TILE - GPSIMD_COLS
 SHARED_TILES = 2
-PLAIN_TILES = M_TILES - SHARED_TILES
 
 FLOPS = 2 * M_TILES * P * CHANNELS * PIXELS
 
@@ -53,7 +50,7 @@ def tile_attention_pa_t_kernel(tc, x, w_phi, w_g, out_0, out_1):
     with ExitStack() as ctx:
         const = ctx.enter_context(tc.tile_pool(name="const", bufs=1))
         raw_pool = ctx.enter_context(tc.tile_pool(name="raw", bufs=1))
-        stream = ctx.enter_context(tc.tile_pool(name="stream", bufs=3))
+        stream = ctx.enter_context(tc.tile_pool(name="stream", bufs=2))
         psum = ctx.enter_context(tc.psum_pool(name="psum", bufs=8))
         ctx.enter_context(tc.manual_schedule())
 
@@ -140,59 +137,53 @@ def tile_attention_pa_t_kernel(tc, x, w_phi, w_g, out_0, out_1):
                 )
             banks[(chunk, m)] = bank
 
-        def pooled_slice(chunk):
-            batch, part = divmod(chunk, CHUNKS_PER_STORE)
-            return pooled[batch][:, :, part * POOLED_TILE : (part + 1) * POOLED_TILE]
-
         def copy_upper_rows(chunk):
             upper_tile = stream.tile([P, SHARED_TILES, POOLED_ROWS, WIDTH], F32, tag="upper")
-            for k in range(SHARED_TILES):
-                rows = banks[(chunk, PLAIN_TILES + k)][:].rearrange("p (i a w) -> p i a w", i=POOLED_ROWS, a=2)
-                nc.scalar.copy(out=upper_tile[:, k], in_=rows[:, :, 0, :])
+            for m in range(SHARED_TILES):
+                rows = banks[(chunk, m)][:].rearrange("p (i a w) -> p i a w", i=POOLED_ROWS, a=2)
+                nc.scalar.copy(out=upper_tile[:, m], in_=rows[:, :, 0, :])
             upper[chunk] = upper_tile
 
         def pool_bank(chunk, m):
-            if chunk % CHUNKS_PER_STORE == 0 and m == 0:
-                pooled_tile = stream.tile([P, M_TILES, STORE_COLS], F32, tag="pooled")
-                pooled[chunk // CHUNKS_PER_STORE] = pooled_tile
-            if m < PLAIN_TILES:
+            if m < SHARED_TILES:
+                rows = banks[(chunk, m)][:].rearrange("p (i a w) -> p i a w", i=POOLED_ROWS, a=2)
+                nc.vector.tensor_tensor(out=upper[chunk][:, m], in0=rows[:, :, 1, :], in1=upper[chunk][:, m], op=MAX)
+            else:
                 nc.vector.tensor_reduce(
-                    out=pooled_slice(chunk)[:, m, :].rearrange("p (i j) -> p i j", i=POOLED_ROWS),
+                    out=pooled[chunk][:, m, :].rearrange("p (i j) -> p i j", i=POOLED_ROWS),
                     in_=banks[(chunk, m)][:].rearrange(
                         "p (i a j b) -> p i j a b", i=POOLED_ROWS, a=2, j=POOLED_WIDTH, b=2
                     ),
                     axis=mybir.AxisListType.XY,
                     op=MAX,
                 )
-            else:
-                k = m - PLAIN_TILES
-                rows = banks[(chunk, m)][:].rearrange("p (i a w) -> p i a w", i=POOLED_ROWS, a=2)
-                nc.vector.tensor_tensor(out=upper[chunk][:, k], in0=rows[:, :, 1, :], in1=upper[chunk][:, k], op=MAX)
 
         def pool_columns(chunk):
-            pairs = upper[chunk][:].rearrange("p k i (j b) -> p k (i j) b", b=2)
+            pairs = upper[chunk][:].rearrange("p m i (j b) -> p m (i j) b", b=2)
             nc.vector.tensor_tensor(
-                out=pooled_slice(chunk)[:, PLAIN_TILES:M_TILES, :], in0=pairs[:, :, :, 0], in1=pairs[:, :, :, 1], op=MAX
+                out=pooled[chunk][:, 0:SHARED_TILES, :], in0=pairs[:, :, :, 0], in1=pairs[:, :, :, 1], op=MAX
             )
 
-        def store(batch):
-            cols = slice(batch * STORE_COLS, (batch + 1) * STORE_COLS)
-            nc.sync.dma_start(out=phi_out[:, cols], in_=pooled[batch][:, 0, :])
-            nc.sync.dma_start(out=g_out[:, :, cols], in_=pooled[batch][:, 1:M_TILES, :])
+        def store(chunk):
+            cols = slice(chunk * POOLED_TILE, (chunk + 1) * POOLED_TILE)
+            nc.sync.dma_start(out=phi_out[:, cols], in_=pooled[chunk][:, 0, :])
+            nc.sync.dma_start(out=g_out[:, :, cols], in_=pooled[chunk][:, 1:M_TILES, :])
 
-        for step in range(-2, CHUNKS + 2):
-            if 0 <= step + 1 < CHUNKS:
-                quantise(step + 1)
-            if step >= 2:
-                pool_columns(step - 2)
-                if (step - 2) % CHUNKS_PER_STORE == CHUNKS_PER_STORE - 1:
-                    store((step - 2) // CHUNKS_PER_STORE)
-            if 1 <= step <= CHUNKS:
-                copy_upper_rows(step - 1)
-            if step + 2 < CHUNKS:
-                regroup(step + 2)
+        for step in range(-2, CHUNKS + 1):
+            if 1 <= step:
+                pooled_tile = stream.tile([P, M_TILES, POOLED_TILE], F32, tag="pooled", bufs=CHUNKS)
+                pooled[step - 1] = pooled_tile
             for m in range(M_TILES):
-                if 1 <= step <= CHUNKS:
+                if 1 <= step:
                     pool_bank(step - 1, m)
                 if 0 <= step < CHUNKS:
                     multiply(step, m)
+            if 1 <= step:
+                pool_columns(step - 1)
+                store(step - 1)
+            if 0 <= step + 1 < CHUNKS:
+                quantise(step + 1)
+            if 0 <= step < CHUNKS:
+                copy_upper_rows(step)
+            if step + 2 < CHUNKS:
+                regroup(step + 2)

@@ -33,6 +33,9 @@ RUN = 4
 GPSIMD_COLS = 320
 SCALAR_COLS = N_TILE - GPSIMD_COLS
 SHARED_TILES = 2
+FINE_CHUNKS = 4
+HEAD_CHUNKS = 2
+HEAD_SCALAR_COLS = N_TILE // 2
 
 FLOPS = 2 * M_TILES * P * CHANNELS * PIXELS
 
@@ -55,9 +58,6 @@ def tile_attention_pa_t_kernel(tc, x, w_phi, w_g, out_0, out_1):
         ctx.enter_context(tc.manual_schedule())
 
         w_rows = const.tile([P, M_TILES, CHANNELS], BF16)
-        nc.sync.dma_start(out=w_rows[:, 0, :], in_=w_phi)
-        for m in range(1, M_TILES):
-            nc.sync.dma_start(out=w_rows[:, m, :], in_=w_g[(m - 1) * P : m * P, :])
         x_rows = x[0].rearrange("(g p j) h w -> g p j (h w)", g=PASSES, p=P, j=PACK)
         raw = {}
 
@@ -70,10 +70,15 @@ def tile_attention_pa_t_kernel(tc, x, w_phi, w_g, out_0, out_1):
                 for part in range(chunks):
                     raw[(first_chunk + part, g)] = raw_tile[:, :, part * N_TILE : (part + 1) * N_TILE]
 
-        for chunk in range(CHUNKS_PER_LOAD):
-            load_x(chunk, 1, "raw_chunk", CHUNKS_PER_LOAD * PASSES)
-        for group in range(1, LOAD_GROUPS):
-            load_x(group * CHUNKS_PER_LOAD, CHUNKS_PER_LOAD, "raw_group", (LOAD_GROUPS - 1) * PASSES)
+        load_x(0, 1, "raw_chunk", FINE_CHUNKS * PASSES)
+        nc.sync.dma_start(out=w_rows[:, 0, :], in_=w_phi)
+        for m in range(1, M_TILES):
+            nc.sync.dma_start(out=w_rows[:, m, :], in_=w_g[(m - 1) * P : m * P, :])
+        for chunk in range(1, FINE_CHUNKS):
+            load_x(chunk, 1, "raw_chunk", FINE_CHUNKS * PASSES)
+        fine_groups = FINE_CHUNKS // CHUNKS_PER_LOAD
+        for group in range(fine_groups, LOAD_GROUPS):
+            load_x(group * CHUNKS_PER_LOAD, CHUNKS_PER_LOAD, "raw_group", (LOAD_GROUPS - fine_groups) * PASSES)
 
         identity = const.tile([P, P], F32)
         make_identity(nc, identity[:])
@@ -82,15 +87,15 @@ def tile_attention_pa_t_kernel(tc, x, w_phi, w_g, out_0, out_1):
         w_grouped_words = w_grouped[:].bitcast(F32)
         w_codes = const.tile([P, M_TILES, PASSES, P], U32, align_bytes=64)
         w_scales = const.tile([P, M_TILES, PASSES, P], U8, align_bytes=64)
-        for m in range(M_TILES):
-            w_bank = psum.tile([P, PASSES, 2, P], F32, tag="bank")
-            for g in range(PASSES):
-                for u in range(2):
-                    nc.tensor.transpose(w_bank[:, g, u, :], w_words[:, m, g, u, :], identity[:])
-            nc.vector.tensor_copy(out=w_grouped_words[:, m], in_=w_bank[:].rearrange("p g u o -> p g o u"))
-            if m >= 1:
-                quantise_weights(nc, w_codes, w_scales, w_grouped, m - 1)
-        quantise_weights(nc, w_codes, w_scales, w_grouped, M_TILES - 1)
+
+        def prepare_weights():
+            for m in range(M_TILES):
+                w_bank = psum.tile([P, PASSES, 2, P], F32, tag="bank")
+                for g in range(PASSES):
+                    for u in range(2):
+                        nc.tensor.transpose(w_bank[:, g, u, :], w_words[:, m, g, u, :], identity[:])
+                nc.scalar.copy(out=w_grouped_words[:, m], in_=w_bank[:].rearrange("p g u o -> p g o u"))
+                quantise_weights(nc, w_codes, w_scales, w_grouped, m)
 
         phi_out = out_0[0]
         g_out = out_1[0].rearrange("(m o) n -> o m n", o=P)
@@ -98,20 +103,28 @@ def tile_attention_pa_t_kernel(tc, x, w_phi, w_g, out_0, out_1):
 
         def regroup(chunk):
             grouped_tile = stream.tile([P, PASSES, N_TILE, PACK], BF16, tag="grouped", align_bytes=64)
-            for g, cols in ((0, N_TILE), (1, SCALAR_COLS)):
+            grouped[chunk] = grouped_tile
+            head = chunk < HEAD_CHUNKS
+            for g, cols in ((0, HEAD_SCALAR_COLS), (1, HEAD_SCALAR_COLS)) if head else ((0, N_TILE), (1, SCALAR_COLS)):
                 nc.scalar.copy(
                     out=grouped_tile[:, g, 0:cols, :].rearrange("p (c i) t -> p c t i", i=RUN),
                     in_=raw[(chunk, g)][:, :, 0:cols].rearrange("p t (c i) -> p c t i", i=RUN),
                 )
-            nc.gpsimd.tensor_scalar(
-                out=grouped_tile[:, 1, SCALAR_COLS:N_TILE, :],
-                in0=raw[(chunk, 1)][:, :, SCALAR_COLS:N_TILE].rearrange("p t n -> p n t"),
-                scalar1=1.0,
-                scalar2=0.0,
-                op0=mybir.AluOpType.mult,
-                op1=mybir.AluOpType.add,
-            )
-            grouped[chunk] = grouped_tile
+            if head:
+                for g in range(PASSES):
+                    nc.vector.tensor_copy(
+                        out=grouped_tile[:, g, HEAD_SCALAR_COLS:N_TILE, :],
+                        in_=raw[(chunk, g)][:, :, HEAD_SCALAR_COLS:N_TILE].rearrange("p t n -> p n t"),
+                    )
+            else:
+                nc.gpsimd.tensor_scalar(
+                    out=grouped_tile[:, 1, SCALAR_COLS:N_TILE, :],
+                    in0=raw[(chunk, 1)][:, :, SCALAR_COLS:N_TILE].rearrange("p t n -> p n t"),
+                    scalar1=1.0,
+                    scalar2=0.0,
+                    op0=mybir.AluOpType.mult,
+                    op1=mybir.AluOpType.add,
+                )
 
         def quantise(chunk):
             codes_tile = stream.tile([P, PASSES, N_TILE], U32, tag="codes", align_bytes=64)
@@ -169,7 +182,11 @@ def tile_attention_pa_t_kernel(tc, x, w_phi, w_g, out_0, out_1):
             nc.sync.dma_start(out=phi_out[:, cols], in_=pooled[chunk][:, 0, :])
             nc.sync.dma_start(out=g_out[:, :, cols], in_=pooled[chunk][:, 1:M_TILES, :])
 
-        for step in range(-2, CHUNKS + 1):
+        regroup(0)
+        quantise(0)
+        prepare_weights()
+        regroup(1)
+        for step in range(0, CHUNKS + 1):
             if 1 <= step:
                 pooled_tile = stream.tile([P, M_TILES, POOLED_TILE], F32, tag="pooled", bufs=CHUNKS)
                 pooled[step - 1] = pooled_tile
@@ -181,7 +198,7 @@ def tile_attention_pa_t_kernel(tc, x, w_phi, w_g, out_0, out_1):
             if 1 <= step:
                 pool_columns(step - 1)
                 store(step - 1)
-            if 0 <= step + 1 < CHUNKS:
+            if step + 1 < CHUNKS:
                 quantise(step + 1)
             if 0 <= step < CHUNKS:
                 copy_upper_rows(step)

@@ -25,15 +25,13 @@ POOLED_ROWS = N_TILE // WIDTH // 2
 POOLED_WIDTH = WIDTH // 2
 POOLED_TILE = POOLED_ROWS * POOLED_WIDTH
 
-CHUNKS_PER_LOAD = 2
-LOAD_COLS = CHUNKS_PER_LOAD * N_TILE
-LOAD_GROUPS = CHUNKS // CHUNKS_PER_LOAD
+LOAD_PLAN = (1, 1, 1, 1, 2, 2, 2, 2, 2, 1, 1)
+assert sum(LOAD_PLAN) == CHUNKS
 
 RUN = 4
 GPSIMD_COLS = 320
 SCALAR_COLS = N_TILE - GPSIMD_COLS
 SHARED_TILES = 2
-FINE_CHUNKS = 4
 HEAD_CHUNKS = 2
 HEAD_SCALAR_COLS = N_TILE // 2
 
@@ -61,24 +59,23 @@ def tile_attention_pa_t_kernel(tc, x, w_phi, w_g, out_0, out_1):
         x_rows = x[0].rearrange("(g p j) h w -> g p j (h w)", g=PASSES, p=P, j=PACK)
         raw = {}
 
-        def load_x(first_chunk, chunks, tag, bufs):
+        def load_x(first_chunk, chunks):
             for g in range(PASSES):
-                raw_tile = raw_pool.tile([P, PACK, chunks * N_TILE], BF16, tag=tag, bufs=bufs)
+                raw_tile = raw_pool.tile(
+                    [P, PACK, chunks * N_TILE], BF16, tag="raw%d" % chunks, bufs=len([n for n in LOAD_PLAN if n == chunks]) * PASSES
+                )
                 nc.sync.dma_start(
                     out=raw_tile[:], in_=x_rows[g, :, :, first_chunk * N_TILE : (first_chunk + chunks) * N_TILE]
                 )
                 for part in range(chunks):
                     raw[(first_chunk + part, g)] = raw_tile[:, :, part * N_TILE : (part + 1) * N_TILE]
 
-        load_x(0, 1, "raw_chunk", FINE_CHUNKS * PASSES)
+        load_x(0, LOAD_PLAN[0])
         nc.sync.dma_start(out=w_rows[:, 0, :], in_=w_phi)
         for m in range(1, M_TILES):
             nc.sync.dma_start(out=w_rows[:, m, :], in_=w_g[(m - 1) * P : m * P, :])
-        for chunk in range(1, FINE_CHUNKS):
-            load_x(chunk, 1, "raw_chunk", FINE_CHUNKS * PASSES)
-        fine_groups = FINE_CHUNKS // CHUNKS_PER_LOAD
-        for group in range(fine_groups, LOAD_GROUPS):
-            load_x(group * CHUNKS_PER_LOAD, CHUNKS_PER_LOAD, "raw_group", (LOAD_GROUPS - fine_groups) * PASSES)
+        for k in range(1, len(LOAD_PLAN)):
+            load_x(sum(LOAD_PLAN[:k]), LOAD_PLAN[k])
 
         identity = const.tile([P, P], F32)
         make_identity(nc, identity[:])

@@ -29,9 +29,11 @@ LOAD_PLAN = (1, 1, 1, 1, 2, 2, 2, 2, 2, 1, 1)
 assert sum(LOAD_PLAN) == CHUNKS
 
 RUN = 4
-GPSIMD_COLS = 320
+GPSIMD_COLS = 352
 SCALAR_COLS = N_TILE - GPSIMD_COLS
-SHARED_TILES = 2
+PAIRS = 1
+TAIL_CHUNKS = 2
+TAIL_PAIRS = 2
 HEAD_CHUNKS = 2
 HEAD_SCALAR_COLS = N_TILE // 2
 
@@ -133,32 +135,48 @@ def tile_attention_pa_t_kernel(tc, x, w_phi, w_g, out_0, out_1):
             )
             codes[chunk], scales[chunk] = codes_tile, scales_tile
 
-        def multiply(chunk, m):
-            bank = psum.tile([P, N_TILE], F32, tag="bank")
+        def shared_pairs(chunk):
+            return TAIL_PAIRS if chunk >= CHUNKS - TAIL_CHUNKS else PAIRS
+
+        def one_group(out, chunk, m, cols):
             for g in range(PASSES):
                 nc.tensor.matmul_mx(
-                    out=bank[:],
+                    out=out,
                     lhsT=w_codes[:, m, g, :].bitcast(FP8X4),
                     lhsT_scale=w_scales[:, m, g, :],
-                    rhs=codes[chunk][:, g, :].bitcast(FP8X4),
-                    rhs_scale=scales[chunk][:, g, :],
+                    rhs=codes[chunk][:, g, cols].bitcast(FP8X4),
+                    rhs_scale=scales[chunk][:, g, cols],
                     start=(g == 0),
                     stop=(g == PASSES - 1),
                 )
-            banks[(chunk, m)] = bank
+
+        def multiply(chunk):
+            for a in range(2):
+                for pair in range(shared_pairs(chunk)):
+                    rows_bank = psum.tile([P, 2, POOLED_ROWS, WIDTH], F32, tag="bank")
+                    for k in range(2):
+                        for i in range(POOLED_ROWS):
+                            row = 2 * i + a
+                            one_group(rows_bank[:, k, i, :], chunk, 2 * pair + k, slice(row * WIDTH, (row + 1) * WIDTH))
+                    banks[(chunk, pair, a)] = rows_bank
+            for m in range(2 * shared_pairs(chunk), M_TILES):
+                bank = psum.tile([P, N_TILE], F32, tag="bank")
+                one_group(bank[:], chunk, m, slice(0, N_TILE))
+                banks[(chunk, m)] = bank
 
         def copy_upper_rows(chunk):
-            upper_tile = stream.tile([P, SHARED_TILES, POOLED_ROWS, WIDTH], F32, tag="upper")
-            for m in range(SHARED_TILES):
-                rows = banks[(chunk, m)][:].rearrange("p (i a w) -> p i a w", i=POOLED_ROWS, a=2)
-                nc.scalar.copy(out=upper_tile[:, m], in_=rows[:, :, 0, :])
+            upper_tile = stream.tile([P, 2 * shared_pairs(chunk), POOLED_ROWS, WIDTH], F32, tag="upper")
+            for pair in range(shared_pairs(chunk)):
+                nc.scalar.copy(out=upper_tile[:, 2 * pair : 2 * pair + 2], in_=banks[(chunk, pair, 0)][:])
             upper[chunk] = upper_tile
 
-        def pool_bank(chunk, m):
-            if m < SHARED_TILES:
-                rows = banks[(chunk, m)][:].rearrange("p (i a w) -> p i a w", i=POOLED_ROWS, a=2)
-                nc.vector.tensor_tensor(out=upper[chunk][:, m], in0=rows[:, :, 1, :], in1=upper[chunk][:, m], op=MAX)
-            else:
+        def pool_rows(chunk):
+            for pair in range(shared_pairs(chunk)):
+                both = upper[chunk][:, 2 * pair : 2 * pair + 2]
+                nc.vector.tensor_tensor(out=both, in0=banks[(chunk, pair, 1)][:], in1=both, op=MAX)
+
+        def pool_banks(chunk):
+            for m in range(2 * shared_pairs(chunk), M_TILES):
                 nc.vector.tensor_reduce(
                     out=pooled[chunk][:, m, :].rearrange("p (i j) -> p i j", i=POOLED_ROWS),
                     in_=banks[(chunk, m)][:].rearrange(
@@ -171,7 +189,7 @@ def tile_attention_pa_t_kernel(tc, x, w_phi, w_g, out_0, out_1):
         def pool_columns(chunk):
             pairs = upper[chunk][:].rearrange("p m i (j b) -> p m (i j) b", b=2)
             nc.vector.tensor_tensor(
-                out=pooled[chunk][:, 0:SHARED_TILES, :], in0=pairs[:, :, :, 0], in1=pairs[:, :, :, 1], op=MAX
+                out=pooled[chunk][:, 0 : 2 * shared_pairs(chunk), :], in0=pairs[:, :, :, 0], in1=pairs[:, :, :, 1], op=MAX
             )
 
         def store(chunk):
@@ -187,17 +205,16 @@ def tile_attention_pa_t_kernel(tc, x, w_phi, w_g, out_0, out_1):
             if 1 <= step:
                 pooled_tile = stream.tile([P, M_TILES, POOLED_TILE], F32, tag="pooled", bufs=CHUNKS)
                 pooled[step - 1] = pooled_tile
-            for m in range(M_TILES):
-                if 1 <= step:
-                    pool_bank(step - 1, m)
-                if 0 <= step < CHUNKS:
-                    multiply(step, m)
+                pool_rows(step - 1)
+            if step < CHUNKS:
+                multiply(step)
             if 1 <= step:
+                pool_banks(step - 1)
                 pool_columns(step - 1)
                 store(step - 1)
             if step + 1 < CHUNKS:
                 quantise(step + 1)
-            if 0 <= step < CHUNKS:
+            if step < CHUNKS:
                 copy_upper_rows(step)
             if step + 2 < CHUNKS:
                 regroup(step + 2)

@@ -27,6 +27,8 @@ POOLED_TILE = POOLED_ROWS * POOLED_WIDTH
 
 LOAD_PLAN = (1, 1, 1, 1, 2, 2, 2, 2, 2, 1, 1)
 assert sum(LOAD_PLAN) == CHUNKS
+STORE_PLAN = (4, 4, 4, 2, 1, 1)
+assert sum(STORE_PLAN) == CHUNKS
 
 RUN = 4
 GPSIMD_COLS = 352
@@ -192,26 +194,41 @@ def tile_attention_pa_t_kernel(tc, x, w_phi, w_g, out_0, out_1):
                 out=pooled[chunk][:, 0 : 2 * shared_pairs(chunk), :], in0=pairs[:, :, :, 0], in1=pairs[:, :, :, 1], op=MAX
             )
 
-        def store(chunk):
-            cols = slice(chunk * POOLED_TILE, (chunk + 1) * POOLED_TILE)
-            nc.sync.dma_start(out=phi_out[:, cols], in_=pooled[chunk][:, 0, :])
-            nc.sync.dma_start(out=g_out[:, :, cols], in_=pooled[chunk][:, 1:M_TILES, :])
+        def new_result_tile(first_chunk, chunks):
+            result_tile = stream.tile(
+                [P, M_TILES, chunks * POOLED_TILE],
+                F32,
+                tag="pooled%d" % chunks,
+                bufs=len([n for n in STORE_PLAN if n == chunks]),
+            )
+            for k in range(chunks):
+                pooled[first_chunk + k] = result_tile[:, :, k * POOLED_TILE : (k + 1) * POOLED_TILE]
+            return result_tile
+
+        def store(first_chunk, chunks, result_tile):
+            cols = slice(first_chunk * POOLED_TILE, (first_chunk + chunks) * POOLED_TILE)
+            nc.sync.dma_start(out=phi_out[:, cols], in_=result_tile[:, 0, :])
+            nc.sync.dma_start(out=g_out[:, :, cols], in_=result_tile[:, 1:M_TILES, :])
 
         regroup(0)
         quantise(0)
         prepare_weights()
         regroup(1)
+        store_starts = [sum(STORE_PLAN[:k]) for k in range(len(STORE_PLAN))]
+        open_store = None
         for step in range(0, CHUNKS + 1):
             if 1 <= step:
-                pooled_tile = stream.tile([P, M_TILES, POOLED_TILE], F32, tag="pooled", bufs=CHUNKS)
-                pooled[step - 1] = pooled_tile
+                if step - 1 in store_starts:
+                    chunks = STORE_PLAN[store_starts.index(step - 1)]
+                    open_store = (step - 1, chunks, new_result_tile(step - 1, chunks))
                 pool_rows(step - 1)
             if step < CHUNKS:
                 multiply(step)
             if 1 <= step:
                 pool_banks(step - 1)
                 pool_columns(step - 1)
-                store(step - 1)
+                if step == open_store[0] + open_store[1]:
+                    store(open_store[0], open_store[1], open_store[2])
             if step + 1 < CHUNKS:
                 quantise(step + 1)
             if step < CHUNKS:

@@ -31,11 +31,9 @@ STORE_PLAN = (4, 4, 4, 2, 1, 1)
 assert sum(STORE_PLAN) == CHUNKS
 
 RUN = 4
-GPSIMD_COLS = 352
+GPSIMD_COLS = 384
 SCALAR_COLS = N_TILE - GPSIMD_COLS
-PAIRS = 1
-TAIL_CHUNKS = 2
-TAIL_PAIRS = 2
+SHARED = 4
 HEAD_CHUNKS = 2
 HEAD_SCALAR_COLS = N_TILE // 2
 
@@ -100,7 +98,7 @@ def tile_attention_pa_t_kernel(tc, x, w_phi, w_g, out_0, out_1):
 
         phi_out = out_0[0]
         g_out = out_1[0].rearrange("(m o) n -> o m n", o=P)
-        grouped, codes, scales, banks, upper, pooled = {}, {}, {}, {}, {}, {}
+        grouped, codes, scales, banks, corner, pooled = {}, {}, {}, {}, {}, {}
 
         def regroup(chunk):
             grouped_tile = stream.tile([P, PASSES, N_TILE, PACK], BF16, tag="grouped", align_bytes=64)
@@ -137,9 +135,6 @@ def tile_attention_pa_t_kernel(tc, x, w_phi, w_g, out_0, out_1):
             )
             codes[chunk], scales[chunk] = codes_tile, scales_tile
 
-        def shared_pairs(chunk):
-            return TAIL_PAIRS if chunk >= CHUNKS - TAIL_CHUNKS else PAIRS
-
         def one_group(out, chunk, m, cols):
             for g in range(PASSES):
                 nc.tensor.matmul_mx(
@@ -153,45 +148,39 @@ def tile_attention_pa_t_kernel(tc, x, w_phi, w_g, out_0, out_1):
                 )
 
         def multiply(chunk):
-            for a in range(2):
-                for pair in range(shared_pairs(chunk)):
-                    rows_bank = psum.tile([P, 2, POOLED_ROWS, WIDTH], F32, tag="bank")
-                    for k in range(2):
-                        for i in range(POOLED_ROWS):
-                            row = 2 * i + a
-                            one_group(rows_bank[:, k, i, :], chunk, 2 * pair + k, slice(row * WIDTH, (row + 1) * WIDTH))
-                    banks[(chunk, pair, a)] = rows_bank
-            for m in range(2 * shared_pairs(chunk), M_TILES):
-                bank = psum.tile([P, N_TILE], F32, tag="bank")
-                one_group(bank[:], chunk, m, slice(0, N_TILE))
-                banks[(chunk, m)] = bank
+            for row in [2 * i + a for a in range(2) for i in range(POOLED_ROWS)]:
+                row_bank = psum.tile([P, SHARED, WIDTH], F32, tag="bank")
+                for m in range(SHARED):
+                    one_group(row_bank[:, m, :], chunk, m, slice(row * WIDTH, (row + 1) * WIDTH))
+                banks[(chunk, row)] = row_bank[:].rearrange("p m (j b) -> p m j b", b=2)
+            bank = psum.tile([P, N_TILE], F32, tag="bank")
+            one_group(bank[:], chunk, SHARED, slice(0, N_TILE))
+            banks[(chunk, "last")] = bank
 
-        def copy_upper_rows(chunk):
-            upper_tile = stream.tile([P, 2 * shared_pairs(chunk), POOLED_ROWS, WIDTH], F32, tag="upper")
-            for pair in range(shared_pairs(chunk)):
-                nc.scalar.copy(out=upper_tile[:, 2 * pair : 2 * pair + 2], in_=banks[(chunk, pair, 0)][:])
-            upper[chunk] = upper_tile
+        def copy_corner(chunk, i):
+            if i == 0:
+                corner_tile = stream.tile([P, POOLED_ROWS, SHARED, POOLED_WIDTH], F32, tag="corner")
+                corner[chunk] = corner_tile
+            nc.scalar.copy(out=corner[chunk][:, i], in_=banks[(chunk, 2 * i)][:, :, :, 0])
 
-        def pool_rows(chunk):
-            for pair in range(shared_pairs(chunk)):
-                both = upper[chunk][:, 2 * pair : 2 * pair + 2]
-                nc.vector.tensor_tensor(out=both, in0=banks[(chunk, pair, 1)][:], in1=both, op=MAX)
-
-        def pool_banks(chunk):
-            for m in range(2 * shared_pairs(chunk), M_TILES):
-                nc.vector.tensor_reduce(
-                    out=pooled[chunk][:, m, :].rearrange("p (i j) -> p i j", i=POOLED_ROWS),
-                    in_=banks[(chunk, m)][:].rearrange(
-                        "p (i a j b) -> p i j a b", i=POOLED_ROWS, a=2, j=POOLED_WIDTH, b=2
-                    ),
-                    axis=mybir.AxisListType.XY,
-                    op=MAX,
+        def pool_shared(chunk, a, b):
+            for i in range(POOLED_ROWS):
+                if (a, b) == (1, 1):
+                    out = pooled[chunk][:, 0:SHARED, i * POOLED_WIDTH : (i + 1) * POOLED_WIDTH]
+                else:
+                    out = corner[chunk][:, i]
+                nc.vector.tensor_tensor(
+                    out=out, in0=banks[(chunk, 2 * i + a)][:, :, :, b], in1=corner[chunk][:, i], op=MAX
                 )
 
-        def pool_columns(chunk):
-            pairs = upper[chunk][:].rearrange("p m i (j b) -> p m (i j) b", b=2)
-            nc.vector.tensor_tensor(
-                out=pooled[chunk][:, 0 : 2 * shared_pairs(chunk), :], in0=pairs[:, :, :, 0], in1=pairs[:, :, :, 1], op=MAX
+        def pool_last(chunk):
+            nc.vector.tensor_reduce(
+                out=pooled[chunk][:, SHARED, :].rearrange("p (i j) -> p i j", i=POOLED_ROWS),
+                in_=banks[(chunk, "last")][:].rearrange(
+                    "p (i a j b) -> p i j a b", i=POOLED_ROWS, a=2, j=POOLED_WIDTH, b=2
+                ),
+                axis=mybir.AxisListType.XY,
+                op=MAX,
             )
 
         def new_result_tile(first_chunk, chunks):
@@ -221,17 +210,20 @@ def tile_attention_pa_t_kernel(tc, x, w_phi, w_g, out_0, out_1):
                 if step - 1 in store_starts:
                     chunks = STORE_PLAN[store_starts.index(step - 1)]
                     open_store = (step - 1, chunks, new_result_tile(step - 1, chunks))
-                pool_rows(step - 1)
+                pool_shared(step - 1, 0, 1)
             if step < CHUNKS:
                 multiply(step)
             if 1 <= step:
-                pool_banks(step - 1)
-                pool_columns(step - 1)
-                if step == open_store[0] + open_store[1]:
-                    store(open_store[0], open_store[1], open_store[2])
+                pool_last(step - 1)
+                pool_shared(step - 1, 1, 0)
             if step + 1 < CHUNKS:
                 quantise(step + 1)
+            if 1 <= step:
+                pool_shared(step - 1, 1, 1)
+                if step == open_store[0] + open_store[1]:
+                    store(open_store[0], open_store[1], open_store[2])
             if step < CHUNKS:
-                copy_upper_rows(step)
+                for i in range(POOLED_ROWS):
+                    copy_corner(step, i)
             if step + 2 < CHUNKS:
                 regroup(step + 2)

@@ -101,23 +101,24 @@ def tile_attention_pa_t_kernel(tc, x, w_phi, w_g, out_0, out_1):
         grouped, codes, scales, banks, corner, pooled = {}, {}, {}, {}, {}, {}
 
         def regroup(chunk):
-            grouped_tile = stream.tile([P, PASSES, N_TILE, PACK], BF16, tag="grouped", align_bytes=64)
-            grouped[chunk] = grouped_tile
+            for g in range(PASSES):
+                grouped_tile = stream.tile([P, N_TILE, PACK], BF16, tag="grouped%d" % g, align_bytes=64)
+                grouped[(chunk, g)] = grouped_tile
             head = chunk < HEAD_CHUNKS
             for g, cols in ((0, HEAD_SCALAR_COLS), (1, HEAD_SCALAR_COLS)) if head else ((0, N_TILE), (1, SCALAR_COLS)):
                 nc.scalar.copy(
-                    out=grouped_tile[:, g, 0:cols, :].rearrange("p (c i) t -> p c t i", i=RUN),
+                    out=grouped[(chunk, g)][:, 0:cols, :].rearrange("p (c i) t -> p c t i", i=RUN),
                     in_=raw[(chunk, g)][:, :, 0:cols].rearrange("p t (c i) -> p c t i", i=RUN),
                 )
             if head:
                 for g in range(PASSES):
                     nc.vector.tensor_copy(
-                        out=grouped_tile[:, g, HEAD_SCALAR_COLS:N_TILE, :],
+                        out=grouped[(chunk, g)][:, HEAD_SCALAR_COLS:N_TILE, :],
                         in_=raw[(chunk, g)][:, :, HEAD_SCALAR_COLS:N_TILE].rearrange("p t n -> p n t"),
                     )
             else:
                 nc.gpsimd.tensor_scalar(
-                    out=grouped_tile[:, 1, SCALAR_COLS:N_TILE, :],
+                    out=grouped[(chunk, 1)][:, SCALAR_COLS:N_TILE, :],
                     in0=raw[(chunk, 1)][:, :, SCALAR_COLS:N_TILE].rearrange("p t n -> p n t"),
                     scalar1=1.0,
                     scalar2=0.0,
@@ -128,11 +129,12 @@ def tile_attention_pa_t_kernel(tc, x, w_phi, w_g, out_0, out_1):
         def quantise(chunk):
             codes_tile = stream.tile([P, PASSES, N_TILE], U32, tag="codes", align_bytes=64)
             scales_tile = stream.tile([P, PASSES, N_TILE], U8, tag="scales", align_bytes=64)
-            nc.vector.quantize_mx(
-                out=codes_tile[:].rearrange("p g n -> p (g n)").bitcast(FP8X4),
-                scales=scales_tile[:].rearrange("p g n -> p (g n)"),
-                in_=grouped[chunk][:].rearrange("p g n t -> p (g n t)"),
-            )
+            for g in range(PASSES) if chunk < HEAD_CHUNKS else reversed(range(PASSES)):
+                nc.vector.quantize_mx(
+                    out=codes_tile[:, g, :].bitcast(FP8X4),
+                    scales=scales_tile[:, g, :],
+                    in_=grouped[(chunk, g)][:].rearrange("p n t -> p (n t)"),
+                )
             codes[chunk], scales[chunk] = codes_tile, scales_tile
 
         def one_group(out, chunk, m, cols):

@@ -31,7 +31,7 @@ STORE_PLAN = (4, 4, 4, 2, 1, 1)
 assert sum(STORE_PLAN) == CHUNKS
 
 RUN = 4
-GPSIMD_COLS = 384
+GPSIMD_COLS = 352
 SCALAR_COLS = N_TILE - GPSIMD_COLS
 SHARED = 4
 HEAD_CHUNKS = 2
@@ -102,7 +102,7 @@ def tile_attention_pa_t_kernel(tc, x, w_phi, w_g, out_0, out_1):
 
         def regroup(chunk):
             for g in range(PASSES):
-                grouped_tile = stream.tile([P, N_TILE, PACK], BF16, tag="grouped%d" % g, align_bytes=64)
+                grouped_tile = stream.tile([P, N_TILE, PACK], BF16, tag="grouped%d" % g, bufs=2 - g, align_bytes=64)
                 grouped[(chunk, g)] = grouped_tile
             head = chunk < HEAD_CHUNKS
             for g, cols in ((0, HEAD_SCALAR_COLS), (1, HEAD_SCALAR_COLS)) if head else ((0, N_TILE), (1, SCALAR_COLS)):

@@ -34,6 +34,7 @@ RUN = 4
 GPSIMD_COLS = 352
 SCALAR_COLS = N_TILE - GPSIMD_COLS
 SHARED = 4
+WARM_UP = 12
 HEAD_CHUNKS = 2
 HEAD_SCALAR_COLS = N_TILE // 2
 
@@ -56,6 +57,16 @@ def tile_attention_pa_t_kernel(tc, x, w_phi, w_g, out_0, out_1):
         stream = ctx.enter_context(tc.tile_pool(name="stream", bufs=2))
         psum = ctx.enter_context(tc.psum_pool(name="psum", bufs=8))
         ctx.enter_context(tc.manual_schedule())
+
+        zeros = const.tile([P, N_TILE], BF16)
+        nc.vector.memset(zeros[:], 0.0)
+        idle_bank = psum.tile([P, N_TILE], F32, tag="bank")
+
+        def multiply_zeros(times):
+            for repeat in range(times):
+                nc.tensor.matmul(out=idle_bank[:], lhsT=zeros[:, 0:P], rhs=zeros[:], start=True, stop=True)
+
+        multiply_zeros(WARM_UP)
 
         w_rows = const.tile([P, M_TILES, CHANNELS], BF16)
         x_rows = x[0].rearrange("(g p j) h w -> g p j (h w)", g=PASSES, p=P, j=PACK)
@@ -93,6 +104,7 @@ def tile_attention_pa_t_kernel(tc, x, w_phi, w_g, out_0, out_1):
                 for g in range(PASSES):
                     for u in range(2):
                         nc.tensor.transpose(w_bank[:, g, u, :], w_words[:, m, g, u, :], identity[:])
+                multiply_zeros(1)
                 nc.scalar.copy(out=w_grouped_words[:, m], in_=w_bank[:].rearrange("p g u o -> p g o u"))
                 quantise_weights(nc, w_codes, w_scales, w_grouped, m)
 

@@ -25,7 +25,7 @@ POOLED_ROWS = N_TILE // WIDTH // 2
 POOLED_WIDTH = WIDTH // 2
 POOLED_TILE = POOLED_ROWS * POOLED_WIDTH
 
-LOAD_PLAN = (1, 1, 1, 1, 2, 2, 2, 2, 2, 1, 1)
+LOAD_PLAN = (1, 1, 1, 1, 1, 1, 1, 1, 2, 2, 2, 1, 1)
 assert sum(LOAD_PLAN) == CHUNKS
 STORE_PLAN = (4, 4, 4, 2, 1, 1)
 assert sum(STORE_PLAN) == CHUNKS
@@ -34,9 +34,9 @@ RUN = 4
 GPSIMD_COLS = 352
 SCALAR_COLS = N_TILE - GPSIMD_COLS
 SHARED = 4
-WARM_UP = 12
+WARM_UP = 10
 HEAD_CHUNKS = 2
-HEAD_SCALAR_COLS = N_TILE // 2
+HEAD_SCALAR_COLS = (256, 192)
 
 FLOPS = 2 * M_TILES * P * CHANNELS * PIXELS
 
@@ -117,7 +117,7 @@ def tile_attention_pa_t_kernel(tc, x, w_phi, w_g, out_0, out_1):
                 grouped_tile = stream.tile([P, N_TILE, PACK], BF16, tag="grouped%d" % g, bufs=2 - g, align_bytes=64)
                 grouped[(chunk, g)] = grouped_tile
             head = chunk < HEAD_CHUNKS
-            for g, cols in ((0, HEAD_SCALAR_COLS), (1, HEAD_SCALAR_COLS)) if head else ((0, N_TILE), (1, SCALAR_COLS)):
+            for g, cols in ((0, HEAD_SCALAR_COLS[chunk]), (1, HEAD_SCALAR_COLS[chunk])) if head else ((0, N_TILE), (1, SCALAR_COLS)):
                 nc.scalar.copy(
                     out=grouped[(chunk, g)][:, 0:cols, :].rearrange("p (c i) t -> p c t i", i=RUN),
                     in_=raw[(chunk, g)][:, :, 0:cols].rearrange("p t (c i) -> p c t i", i=RUN),
@@ -125,10 +125,10 @@ def tile_attention_pa_t_kernel(tc, x, w_phi, w_g, out_0, out_1):
             if head:
                 for g in range(PASSES):
                     nc.vector.tensor_copy(
-                        out=grouped[(chunk, g)][:, HEAD_SCALAR_COLS:N_TILE, :],
-                        in_=raw[(chunk, g)][:, :, HEAD_SCALAR_COLS:N_TILE].rearrange("p t n -> p n t"),
+                        out=grouped[(chunk, g)][:, HEAD_SCALAR_COLS[chunk] : N_TILE, :],
+                        in_=raw[(chunk, g)][:, :, HEAD_SCALAR_COLS[chunk] : N_TILE].rearrange("p t n -> p n t"),
                     )
-            else:
+            elif chunk > HEAD_CHUNKS:
                 nc.gpsimd.tensor_scalar(
                     out=grouped[(chunk, 1)][:, SCALAR_COLS:N_TILE, :],
                     in0=raw[(chunk, 1)][:, :, SCALAR_COLS:N_TILE].rearrange("p t n -> p n t"),
@@ -138,10 +138,16 @@ def tile_attention_pa_t_kernel(tc, x, w_phi, w_g, out_0, out_1):
                     op1=mybir.AluOpType.add,
                 )
 
+        def regroup_third_chunk():
+            nc.vector.tensor_copy(
+                out=grouped[(HEAD_CHUNKS, 1)][:, SCALAR_COLS:N_TILE, :],
+                in_=raw[(HEAD_CHUNKS, 1)][:, :, SCALAR_COLS:N_TILE].rearrange("p t n -> p n t"),
+            )
+
         def quantise(chunk):
             codes_tile = stream.tile([P, PASSES, N_TILE], U32, tag="codes", align_bytes=64)
             scales_tile = stream.tile([P, PASSES, N_TILE], U8, tag="scales", align_bytes=64)
-            for g in range(PASSES) if chunk < HEAD_CHUNKS else reversed(range(PASSES)):
+            for g in range(PASSES) if chunk <= HEAD_CHUNKS else reversed(range(PASSES)):
                 nc.vector.quantize_mx(
                     out=codes_tile[:, g, :].bitcast(FP8X4),
                     scales=scales_tile[:, g, :],
@@ -208,10 +214,15 @@ def tile_attention_pa_t_kernel(tc, x, w_phi, w_g, out_0, out_1):
                 pooled[first_chunk + k] = result_tile[:, :, k * POOLED_TILE : (k + 1) * POOLED_TILE]
             return result_tile
 
-        def store(first_chunk, chunks, result_tile):
+        def store_group(first_chunk, chunks, result_tile):
             cols = slice(first_chunk * POOLED_TILE, (first_chunk + chunks) * POOLED_TILE)
-            nc.sync.dma_start(out=phi_out[:, cols], in_=result_tile[:, 0, :])
-            nc.sync.dma_start(out=g_out[:, :, cols], in_=result_tile[:, 1:M_TILES, :])
+            if first_chunk + chunks < CHUNKS:
+                nc.sync.dma_start(out=phi_out[:, cols], in_=result_tile[:, 0, :])
+                nc.sync.dma_start(out=g_out[:, :, cols], in_=result_tile[:, 1:M_TILES, :])
+            else:
+                nc.sync.dma_start(out=g_out[:, SHARED - 1, cols], in_=result_tile[:, SHARED, :])
+                nc.scalar.dma_start(out=phi_out[:, cols], in_=result_tile[:, 0, :])
+                nc.sync.dma_start(out=g_out[:, 0 : SHARED - 1, cols], in_=result_tile[:, 1:SHARED, :])
 
         regroup(0)
         quantise(0)
@@ -230,12 +241,14 @@ def tile_attention_pa_t_kernel(tc, x, w_phi, w_g, out_0, out_1):
             if 1 <= step:
                 pool_last(step - 1)
                 pool_shared(step - 1, 1, 0)
+            if step + 1 == HEAD_CHUNKS:
+                regroup_third_chunk()
             if step + 1 < CHUNKS:
                 quantise(step + 1)
             if 1 <= step:
                 pool_shared(step - 1, 1, 1)
                 if step == open_store[0] + open_store[1]:
-                    store(open_store[0], open_store[1], open_store[2])
+                    store_group(open_store[0], open_store[1], open_store[2])
             if step < CHUNKS:
                 for i in range(POOLED_ROWS):
                     copy_corner(step, i)

@@ -114,7 +114,7 @@ def tile_attention_pa_t_kernel(tc, x, w_phi, w_g, out_0, out_1):
 
         def regroup(chunk):
             for g in range(PASSES):
-                grouped_tile = stream.tile([P, N_TILE, PACK], BF16, tag="grouped%d" % g, bufs=2 - g, align_bytes=64)
+                grouped_tile = stream.tile([P, N_TILE, PACK], BF16, tag="grouped%d" % g, bufs=(3, 1)[g], align_bytes=64)
                 grouped[(chunk, g)] = grouped_tile
             head = chunk < HEAD_CHUNKS
             for g, cols in ((0, HEAD_SCALAR_COLS[chunk]), (1, HEAD_SCALAR_COLS[chunk])) if head else ((0, N_TILE), (1, SCALAR_COLS)):
@@ -179,7 +179,7 @@ def tile_attention_pa_t_kernel(tc, x, w_phi, w_g, out_0, out_1):
 
         def copy_corner(chunk, i):
             if i == 0:
-                corner_tile = stream.tile([P, POOLED_ROWS, SHARED, POOLED_WIDTH], F32, tag="corner")
+                corner_tile = stream.tile([P, POOLED_ROWS, SHARED, POOLED_WIDTH], F32, tag="corner", bufs=3)
                 corner[chunk] = corner_tile
             nc.scalar.copy(out=corner[chunk][:, i], in_=banks[(chunk, 2 * i)][:, :, :, 0])
 

from contextlib import ExitStack

import concourse.mybir as mybir
from concourse.masks import make_identity

BF16 = mybir.dt.bfloat16
F32 = mybir.dt.float32
U32 = mybir.dt.uint32
U8 = mybir.dt.uint8
FP8X4 = mybir.dt.float8_e4m3fn_x4
MAX = mybir.AluOpType.max

P = 128
PACK = 4
K_PASS = P * PACK

CHANNELS, HEIGHT, WIDTH = 1024, 64, 128
PIXELS = HEIGHT * WIDTH
PASSES = CHANNELS // K_PASS
M_TILES = 5

N_TILE = 512
CHUNKS = PIXELS // N_TILE
POOLED_ROWS = N_TILE // WIDTH // 2
POOLED_WIDTH = WIDTH // 2
POOLED_TILE = POOLED_ROWS * POOLED_WIDTH

LOAD_PLAN = (1, 1, 1, 1, 1, 1, 1, 1, 2, 2, 2, 1, 1)
assert sum(LOAD_PLAN) == CHUNKS
STORE_PLAN = (4, 4, 4, 2, 1, 1)
assert sum(STORE_PLAN) == CHUNKS

RUN = 4
GPSIMD_COLS = 352
SCALAR_COLS = N_TILE - GPSIMD_COLS
SHARED = 4
WARM_UP = 10
HEAD_CHUNKS = 2
HEAD_SCALAR_COLS = (256, 192)

FLOPS = 2 * M_TILES * P * CHANNELS * PIXELS


def quantise_weights(nc, w_codes, w_scales, w_grouped, m):
    nc.vector.quantize_mx(
        out=w_codes[:, m].rearrange("p g o -> p (g o)").bitcast(FP8X4),
        scales=w_scales[:, m].rearrange("p g o -> p (g o)"),
        in_=w_grouped[:, m].rearrange("p g o t -> p (g o t)"),
    )


def tile_attention_pa_t_kernel(tc, x, w_phi, w_g, out_0, out_1):
    nc = tc.nc
    with ExitStack() as ctx:
        const = ctx.enter_context(tc.tile_pool(name="const", bufs=1))
        raw_pool = ctx.enter_context(tc.tile_pool(name="raw", bufs=1))
        stream = ctx.enter_context(tc.tile_pool(name="stream", bufs=2))
        psum = ctx.enter_context(tc.psum_pool(name="psum", bufs=8))
        ctx.enter_context(tc.manual_schedule())

        zeros = const.tile([P, N_TILE], BF16)
        nc.vector.memset(zeros[:], 0.0)
        idle_bank = psum.tile([P, N_TILE], F32, tag="bank")

        def multiply_zeros(times):
            for repeat in range(times):
                nc.tensor.matmul(out=idle_bank[:], lhsT=zeros[:, 0:P], rhs=zeros[:], start=True, stop=True)

        multiply_zeros(WARM_UP)

        w_rows = const.tile([P, M_TILES, CHANNELS], BF16)
        x_rows = x[0].rearrange("(g p j) h w -> g p j (h w)", g=PASSES, p=P, j=PACK)
        raw = {}

        def load_x(first_chunk, chunks):
            for g in range(PASSES):
                raw_tile = raw_pool.tile(
                    [P, PACK, chunks * N_TILE], BF16, tag="raw%d" % chunks, bufs=len([n for n in LOAD_PLAN if n == chunks]) * PASSES
                )
                nc.sync.dma_start(
                    out=raw_tile[:], in_=x_rows[g, :, :, first_chunk * N_TILE : (first_chunk + chunks) * N_TILE]
                )
                for part in range(chunks):
                    raw[(first_chunk + part, g)] = raw_tile[:, :, part * N_TILE : (part + 1) * N_TILE]

        load_x(0, LOAD_PLAN[0])
        nc.sync.dma_start(out=w_rows[:, 0, :], in_=w_phi)
        for m in range(1, M_TILES):
            nc.sync.dma_start(out=w_rows[:, m, :], in_=w_g[(m - 1) * P : m * P, :])
        for k in range(1, len(LOAD_PLAN)):
            load_x(sum(LOAD_PLAN[:k]), LOAD_PLAN[k])

        identity = const.tile([P, P], F32)
        make_identity(nc, identity[:])
        w_words = w_rows[:].bitcast(F32).rearrange("o m (g p u) -> o m g u p", g=PASSES, p=P, u=2)
        w_grouped = const.tile([P, M_TILES, PASSES, P, PACK], BF16, align_bytes=64)
        w_grouped_words = w_grouped[:].bitcast(F32)
        w_codes = const.tile([P, M_TILES, PASSES, P], U32, align_bytes=64)
        w_scales = const.tile([P, M_TILES, PASSES, P], U8, align_bytes=64)

        def prepare_weights():
            for m in range(M_TILES):
                w_bank = psum.tile([P, PASSES, 2, P], F32, tag="bank")
                for g in range(PASSES):
                    for u in range(2):
                        nc.tensor.transpose(w_bank[:, g, u, :], w_words[:, m, g, u, :], identity[:])
                multiply_zeros(1)
                nc.scalar.copy(out=w_grouped_words[:, m], in_=w_bank[:].rearrange("p g u o -> p g o u"))
                quantise_weights(nc, w_codes, w_scales, w_grouped, m)

        phi_out = out_0[0]
        g_out = out_1[0].rearrange("(m o) n -> o m n", o=P)
        grouped, codes, scales, banks, corner, pooled = {}, {}, {}, {}, {}, {}

        def regroup(chunk):
            for g in range(PASSES):
                grouped_tile = stream.tile([P, N_TILE, PACK], BF16, tag="grouped%d" % g, bufs=(3, 1)[g], align_bytes=64)
                grouped[(chunk, g)] = grouped_tile
            head = chunk < HEAD_CHUNKS
            for g, cols in ((0, HEAD_SCALAR_COLS[chunk]), (1, HEAD_SCALAR_COLS[chunk])) if head else ((0, N_TILE), (1, SCALAR_COLS)):
                nc.scalar.copy(
                    out=grouped[(chunk, g)][:, 0:cols, :].rearrange("p (c i) t -> p c t i", i=RUN),
                    in_=raw[(chunk, g)][:, :, 0:cols].rearrange("p t (c i) -> p c t i", i=RUN),
                )
            if head:
                for g in range(PASSES):
                    nc.vector.tensor_copy(
                        out=grouped[(chunk, g)][:, HEAD_SCALAR_COLS[chunk] : N_TILE, :],
                        in_=raw[(chunk, g)][:, :, HEAD_SCALAR_COLS[chunk] : N_TILE].rearrange("p t n -> p n t"),
                    )
            elif chunk > HEAD_CHUNKS:
                nc.gpsimd.tensor_scalar(
                    out=grouped[(chunk, 1)][:, SCALAR_COLS:N_TILE, :],
                    in0=raw[(chunk, 1)][:, :, SCALAR_COLS:N_TILE].rearrange("p t n -> p n t"),
                    scalar1=1.0,
                    scalar2=0.0,
                    op0=mybir.AluOpType.mult,
                    op1=mybir.AluOpType.add,
                )

        def regroup_third_chunk():
            nc.vector.tensor_copy(
                out=grouped[(HEAD_CHUNKS, 1)][:, SCALAR_COLS:N_TILE, :],
                in_=raw[(HEAD_CHUNKS, 1)][:, :, SCALAR_COLS:N_TILE].rearrange("p t n -> p n t"),
            )

        def quantise(chunk):
            codes_tile = stream.tile([P, PASSES, N_TILE], U32, tag="codes", align_bytes=64)
            scales_tile = stream.tile([P, PASSES, N_TILE], U8, tag="scales", align_bytes=64)
            for g in range(PASSES) if chunk <= HEAD_CHUNKS else reversed(range(PASSES)):
                nc.vector.quantize_mx(
                    out=codes_tile[:, g, :].bitcast(FP8X4),
                    scales=scales_tile[:, g, :],
                    in_=grouped[(chunk, g)][:].rearrange("p n t -> p (n t)"),
                )
            codes[chunk], scales[chunk] = codes_tile, scales_tile

        def one_group(out, chunk, m, cols):
            for g in range(PASSES):
                nc.tensor.matmul_mx(
                    out=out,
                    lhsT=w_codes[:, m, g, :].bitcast(FP8X4),
                    lhsT_scale=w_scales[:, m, g, :],
                    rhs=codes[chunk][:, g, cols].bitcast(FP8X4),
                    rhs_scale=scales[chunk][:, g, cols],
                    start=(g == 0),
                    stop=(g == PASSES - 1),
                )

        def multiply(chunk):
            for row in [2 * i + a for a in range(2) for i in range(POOLED_ROWS)]:
                row_bank = psum.tile([P, SHARED, WIDTH], F32, tag="bank")
                for m in range(SHARED):
                    one_group(row_bank[:, m, :], chunk, m, slice(row * WIDTH, (row + 1) * WIDTH))
                banks[(chunk, row)] = row_bank[:].rearrange("p m (j b) -> p m j b", b=2)
            bank = psum.tile([P, N_TILE], F32, tag="bank")
            one_group(bank[:], chunk, SHARED, slice(0, N_TILE))
            banks[(chunk, "last")] = bank

        def copy_corner(chunk, i):
            if i == 0:
                corner_tile = stream.tile([P, POOLED_ROWS, SHARED, POOLED_WIDTH], F32, tag="corner", bufs=3)
                corner[chunk] = corner_tile
            nc.scalar.copy(out=corner[chunk][:, i], in_=banks[(chunk, 2 * i)][:, :, :, 0])

        def pool_shared(chunk, a, b):
            for i in range(POOLED_ROWS):
                if (a, b) == (1, 1):
                    out = pooled[chunk][:, 0:SHARED, i * POOLED_WIDTH : (i + 1) * POOLED_WIDTH]
                else:
                    out = corner[chunk][:, i]
                nc.vector.tensor_tensor(
                    out=out, in0=banks[(chunk, 2 * i + a)][:, :, :, b], in1=corner[chunk][:, i], op=MAX
                )

        def pool_last(chunk):
            nc.vector.tensor_reduce(
                out=pooled[chunk][:, SHARED, :].rearrange("p (i j) -> p i j", i=POOLED_ROWS),
                in_=banks[(chunk, "last")][:].rearrange(
                    "p (i a j b) -> p i j a b", i=POOLED_ROWS, a=2, j=POOLED_WIDTH, b=2
                ),
                axis=mybir.AxisListType.XY,
                op=MAX,
            )

        def new_result_tile(first_chunk, chunks):
            result_tile = stream.tile(
                [P, M_TILES, chunks * POOLED_TILE],
                F32,
                tag="pooled%d" % chunks,
                bufs=len([n for n in STORE_PLAN if n == chunks]),
            )
            for k in range(chunks):
                pooled[first_chunk + k] = result_tile[:, :, k * POOLED_TILE : (k + 1) * POOLED_TILE]
            return result_tile

        def store_group(first_chunk, chunks, result_tile):
            cols = slice(first_chunk * POOLED_TILE, (first_chunk + chunks) * POOLED_TILE)
            if first_chunk + chunks < CHUNKS:
                nc.sync.dma_start(out=phi_out[:, cols], in_=result_tile[:, 0, :])
                nc.sync.dma_start(out=g_out[:, :, cols], in_=result_tile[:, 1:M_TILES, :])
            else:
                nc.sync.dma_start(out=g_out[:, SHARED - 1, cols], in_=result_tile[:, SHARED, :])
                nc.scalar.dma_start(out=phi_out[:, cols], in_=result_tile[:, 0, :])
                nc.sync.dma_start(out=g_out[:, 0 : SHARED - 1, cols], in_=result_tile[:, 1:SHARED, :])

        regroup(0)
        quantise(0)
        prepare_weights()
        regroup(1)
        store_starts = [sum(STORE_PLAN[:k]) for k in range(len(STORE_PLAN))]
        open_store = None
        for step in range(0, CHUNKS + 1):
            if 1 <= step:
                if step - 1 in store_starts:
                    chunks = STORE_PLAN[store_starts.index(step - 1)]
                    open_store = (step - 1, chunks, new_result_tile(step - 1, chunks))
                pool_shared(step - 1, 0, 1)
            if step < CHUNKS:
                multiply(step)
            if 1 <= step:
                pool_last(step - 1)
                pool_shared(step - 1, 1, 0)
            if step + 1 == HEAD_CHUNKS:
                regroup_third_chunk()
            if step + 1 < CHUNKS:
                quantise(step + 1)
            if 1 <= step:
                pool_shared(step - 1, 1, 1)
                if step == open_store[0] + open_store[1]:
                    store_group(open_store[0], open_store[1], open_store[2])
            if step < CHUNKS:
                for i in range(POOLED_ROWS):
                    copy_corner(step, i)
            if step + 2 < CHUNKS:
                regroup(step + 2)
